import numpy as np
import ml_dtypes

BF16 = ml_dtypes.bfloat16


def bf(x):
    return np.asarray(x, np.float32).astype(BF16)


def f32(x):
    return np.asarray(x, np.float32)


def f64(x):
    return np.asarray(x).astype(np.float64)


def striped(idx):
    return np.tile(idx.reshape(-1, 16).T, (8, 1))


S, D, NH, N = 256, 128, 256, 128


def setup_inputs():
    return {"table": bf(np.random.standard_normal((D, S))), "bnode": f32(0.1 * np.random.standard_normal((D, 1))), "pos": bf(np.random.standard_normal((D, N))), "wv": bf(np.random.standard_normal((NH, NH)) / np.sqrt(NH)), "bv": f32(0.1 * np.random.standard_normal((NH, 1))), "wo": bf(np.random.standard_normal((NH, NH)) / np.sqrt(NH)), "bo": f32(0.1 * np.random.standard_normal((NH, 1))), "offs": striped(np.random.permutation(np.tile(np.arange(S), 2))[:N])}


def reference(table, bnode, pos, wv, bv, wo, bo, offs):
    idx = offs[:16].T.reshape(-1)
    feat = np.maximum(f64(table) + f64(bnode), 0.0)
    x = np.concatenate([feat[:, idx], f64(pos)], axis=0)
    v = f64(wv).T @ x + f64(bv)
    return x + f64(wo).T @ v + f64(bo)

@@ -1,0 +1,79 @@
+import concourse.mybir as mybir
+from concourse.masks import make_identity
+
+P = 128
+S = 256
+N = 128
+NH = 256
+NB = NH // P
+
+FLOPS = 2 * 2 * NH * NH * N
+
+BF16, F32, U16 = mybir.dt.bfloat16, mybir.dt.float32, mybir.dt.uint16
+ADD, MAX = mybir.AluOpType.add, mybir.AluOpType.max
+IDENTITY = mybir.ActivationFunctionType.Identity
+
+
+def block(b):
+    return slice(b * P, (b + 1) * P)
+
+
+def tile_pace_nodagseq_kernel(tc, table, bnode, pos, wv, bv, wo, bo, offs, out):
+    nc = tc.nc
+    with (
+        tc.tile_pool(name="held", bufs=1) as held,
+        tc.psum_pool(name="psum", bufs=1) as psum,
+    ):
+        offsets = held.tile([P, N // 16], U16, name="offsets")
+        table_sb = held.tile([P, S], BF16, name="table_sb")
+        bnode_sb = held.tile([P, 1], F32, name="bnode_sb")
+        pos_sb = held.tile([P, N], BF16, name="pos_sb")
+        wv_sb = [held.tile([P, NH], BF16, name=f"wv_sb{cb}") for cb in range(NB)]
+        wo_sb = [held.tile([P, NH], BF16, name=f"wo_sb{hb}") for hb in range(NB)]
+        bv_sb = held.tile([P, NB], F32, name="bv_sb")
+        bo_sb = held.tile([P, NB], F32, name="bo_sb")
+
+        nc.sync.dma_start(table_sb[:], table)
+        nc.sync.dma_start(offsets[:], offs)
+        nc.sync.dma_start(wv_sb[0][:], wv[block(0), :])
+        nc.sync.dma_start(wo_sb[0][:], wo[block(0), :])
+        nc.scalar.dma_start(bnode_sb[:], bnode)
+        nc.scalar.dma_start(pos_sb[:], pos)
+        nc.scalar.dma_start(wv_sb[1][:], wv[block(1), :])
+        nc.scalar.dma_start(wo_sb[1][:], wo[block(1), :])
+        with nc.allow_non_contiguous_dma(reason="a bias: one float32 to a partition and block"):
+            nc.gpsimd.dma_start(bv_sb[:], bv.rearrange("(b p) o -> p (b o)", p=P))
+            nc.gpsimd.dma_start(bo_sb[:], bo.rearrange("(b p) o -> p (b o)", p=P))
+
+        identity = held.tile([P, P], BF16, name="identity")
+        make_identity(nc, identity[:])
+
+        feat = held.tile([P, S], BF16, name="feat")
+        nc.vector.tensor_scalar(feat[:], table_sb[:], bnode_sb[:, 0:1], 0.0, op0=ADD, op1=MAX)
+
+        v_ps = [psum.tile([P, N], F32, name=f"v_ps{hb}") for hb in range(NB)]
+        for hb in range(NB):
+            nc.tensor.matmul(v_ps[hb][:], wv_sb[1][:, block(hb)], pos_sb[:], start=True, stop=False)
+        for hb in range(NB):
+            nc.tensor.matmul(
+                v_ps[hb][:], wv_sb[0][:, block(hb)], feat[:].indirect(offsets[:]), start=False, stop=True
+            )
+
+        out_ps = [psum.tile([P, N], F32, name=f"out_ps{mb}") for mb in range(NB)]
+        nc.tensor.matmul(out_ps[0][:], identity[:], feat[:].indirect(offsets[:]), start=True, stop=False)
+        nc.tensor.matmul(out_ps[1][:], identity[:], pos_sb[:], start=True, stop=False)
+
+        v_sb = [held.tile([P, N], BF16, name=f"v_sb{hb}") for hb in range(NB)]
+        nc.vector.tensor_scalar_add(v_sb[0][:], v_ps[0][:], bv_sb[:, 0:1])
+        nc.scalar.activation(v_sb[1][:], v_ps[1][:], IDENTITY, bias=bv_sb[:, 1:2])
+
+        for mb in range(NB):
+            for hb in range(NB):
+                nc.tensor.matmul(
+                    out_ps[mb][:], wo_sb[hb][:, block(mb)], v_sb[hb][:], start=False, stop=(hb == NB - 1)
+                )
+        out_sb = [held.tile([P, N], F32, name=f"out_sb{mb}") for mb in range(NB)]
+        nc.vector.tensor_scalar_add(out_sb[0][:], out_ps[0][:], bo_sb[:, 0:1])
+        nc.scalar.activation(out_sb[1][:], out_ps[1][:], IDENTITY, bias=bo_sb[:, 1:2])
+        nc.sync.dma_start(out[block(0), :], out_sb[0][:])
+        nc.scalar.dma_start(out[block(1), :], out_sb[1][:])

@@ -11,7 +11,6 @@ FLOPS = 2 * 2 * NH * NH * N
 
 BF16, F32, U16 = mybir.dt.bfloat16, mybir.dt.float32, mybir.dt.uint16
 ADD, MAX = mybir.AluOpType.add, mybir.AluOpType.max
-IDENTITY = mybir.ActivationFunctionType.Identity
 
 
 def block(b):
@@ -64,8 +63,8 @@ def tile_pace_nodagseq_kernel(tc, table, bnode, pos, wv, bv, wo, bo, offs, out):
         nc.tensor.matmul(out_ps[1][:], identity[:], pos_sb[:], start=True, stop=False)
 
         v_sb = [held.tile([P, N], BF16, name=f"v_sb{hb}") for hb in range(NB)]
-        nc.vector.tensor_scalar_add(v_sb[0][:], v_ps[0][:], bv_sb[:, 0:1])
-        nc.scalar.activation(v_sb[1][:], v_ps[1][:], IDENTITY, bias=bv_sb[:, 1:2])
+        for hb in range(NB):
+            nc.vector.tensor_scalar_add(v_sb[hb][:], v_ps[hb][:], bv_sb[:, hb : hb + 1])
 
         for mb in range(NB):
             for hb in range(NB):
@@ -73,7 +72,7 @@ def tile_pace_nodagseq_kernel(tc, table, bnode, pos, wv, bv, wo, bo, offs, out):
                     out_ps[mb][:], wo_sb[hb][:, block(mb)], v_sb[hb][:], start=False, stop=(hb == NB - 1)
                 )
         out_sb = [held.tile([P, N], F32, name=f"out_sb{mb}") for mb in range(NB)]
-        nc.vector.tensor_scalar_add(out_sb[0][:], out_ps[0][:], bo_sb[:, 0:1])
-        nc.scalar.activation(out_sb[1][:], out_ps[1][:], IDENTITY, bias=bo_sb[:, 1:2])
+        for mb in range(NB):
+            nc.vector.tensor_scalar_add(out_sb[mb][:], out_ps[mb][:], bo_sb[:, mb : mb + 1])
         nc.sync.dma_start(out[block(0), :], out_sb[0][:])
         nc.scalar.dma_start(out[block(1), :], out_sb[1][:])

@@ -27,22 +27,20 @@ def tile_pace_nodagseq_kernel(tc, table, bnode, pos, wv, bv, wo, bo, offs, out):
         table_sb = held.tile([P, S], BF16, name="table_sb")
         bnode_sb = held.tile([P, 1], F32, name="bnode_sb")
         pos_sb = held.tile([P, N], BF16, name="pos_sb")
-        wv_sb = [held.tile([P, NH], BF16, name=f"wv_sb{cb}") for cb in range(NB)]
-        wo_sb = [held.tile([P, NH], BF16, name=f"wo_sb{hb}") for hb in range(NB)]
+        wv_sb = held.tile([P, NB, NH], BF16, name="wv_sb")
+        wo_sb = held.tile([P, NB, NH], BF16, name="wo_sb")
         bv_sb = held.tile([P, NB], F32, name="bv_sb")
         bo_sb = held.tile([P, NB], F32, name="bo_sb")
 
         nc.sync.dma_start(table_sb[:], table)
-        nc.sync.dma_start(offsets[:], offs)
-        nc.sync.dma_start(wv_sb[0][:], wv[block(0), :])
-        nc.sync.dma_start(wo_sb[0][:], wo[block(0), :])
         nc.scalar.dma_start(bnode_sb[:], bnode)
-        nc.scalar.dma_start(pos_sb[:], pos)
-        nc.scalar.dma_start(wv_sb[1][:], wv[block(1), :])
-        nc.scalar.dma_start(wo_sb[1][:], wo[block(1), :])
+        nc.sync.dma_start(offsets[:], offs)
+        nc.scalar.dma_start(wv_sb[:], wv.rearrange("(b p) h -> p b h", p=P))
+        nc.sync.dma_start(pos_sb[:], pos)
+        nc.sync.dma_start(wo_sb[:], wo.rearrange("(b p) m -> p b m", p=P))
         with nc.allow_non_contiguous_dma(reason="a bias: one float32 to a partition and block"):
-            nc.gpsimd.dma_start(bv_sb[:], bv.rearrange("(b p) o -> p (b o)", p=P))
-            nc.gpsimd.dma_start(bo_sb[:], bo.rearrange("(b p) o -> p (b o)", p=P))
+            nc.scalar.dma_start(bv_sb[:], bv.rearrange("(b p) o -> p (b o)", p=P))
+            nc.scalar.dma_start(bo_sb[:], bo.rearrange("(b p) o -> p (b o)", p=P))
 
         identity = held.tile([P, P], BF16, name="identity")
         make_identity(nc, identity[:])
@@ -52,10 +50,10 @@ def tile_pace_nodagseq_kernel(tc, table, bnode, pos, wv, bv, wo, bo, offs, out):
 
         v_ps = [psum.tile([P, N], F32, name=f"v_ps{hb}") for hb in range(NB)]
         for hb in range(NB):
-            nc.tensor.matmul(v_ps[hb][:], wv_sb[1][:, block(hb)], pos_sb[:], start=True, stop=False)
+            nc.tensor.matmul(v_ps[hb][:], wv_sb[:, 1, block(hb)], pos_sb[:], start=True, stop=False)
         for hb in range(NB):
             nc.tensor.matmul(
-                v_ps[hb][:], wv_sb[0][:, block(hb)], feat[:].indirect(offsets[:]), start=False, stop=True
+                v_ps[hb][:], wv_sb[:, 0, block(hb)], feat[:].indirect(offsets[:]), start=False, stop=True
             )
 
         out_ps = [psum.tile([P, N], F32, name=f"out_ps{mb}") for mb in range(NB)]
@@ -69,7 +67,7 @@ def tile_pace_nodagseq_kernel(tc, table, bnode, pos, wv, bv, wo, bo, offs, out):
         for mb in range(NB):
             for hb in range(NB):
                 nc.tensor.matmul(
-                    out_ps[mb][:], wo_sb[hb][:, block(mb)], v_sb[hb][:], start=False, stop=(hb == NB - 1)
+                    out_ps[mb][:], wo_sb[:, hb, block(mb)], v_sb[hb][:], start=False, stop=(hb == NB - 1)
                 )
         out_sb = [held.tile([P, N], F32, name=f"out_sb{mb}") for mb in range(NB)]
         for mb in range(NB):

@@ -64,8 +64,8 @@ def tile_pace_nodagseq_kernel(tc, table, bnode, pos, wv, bv, wo, bo, offs, out):
         for hb in range(NB):
             nc.vector.tensor_scalar_add(v_sb[hb][:], v_ps[hb][:], bv_sb[:, hb : hb + 1])
 
-        for mb in range(NB):
-            for hb in range(NB):
+        for hb in range(NB):
+            for mb in range(NB):
                 nc.tensor.matmul(
                     out_ps[mb][:], wo_sb[:, hb, block(mb)], v_sb[hb][:], start=False, stop=(hb == NB - 1)
                 )

@@ -7,6 +7,9 @@ N = 128
 NH = 256
 NB = NH // P
 
+WARM_COLUMNS = 512
+WARM_MATMULS = 4
+
 FLOPS = 2 * 2 * NH * NH * N
 
 BF16, F32, U16 = mybir.dt.bfloat16, mybir.dt.float32, mybir.dt.uint16
@@ -45,6 +48,12 @@ def tile_pace_nodagseq_kernel(tc, table, bnode, pos, wv, bv, wo, bo, offs, out):
         identity = held.tile([P, P], BF16, name="identity")
         make_identity(nc, identity[:])
 
+        warm_sb = held.tile([P, WARM_COLUMNS], BF16, name="warm_sb")
+        warm_ps = psum.tile([P, WARM_COLUMNS], F32, name="warm_ps")
+        nc.vector.memset(warm_sb[:], 0.0)
+        for i in range(WARM_MATMULS):
+            nc.tensor.matmul(warm_ps[:], warm_sb[:, 0:P], warm_sb[:], start=True, stop=True)
+
         feat = held.tile([P, S], BF16, name="feat")
         nc.vector.tensor_scalar(feat[:], table_sb[:], bnode_sb[:, 0:1], 0.0, op0=ADD, op1=MAX)
 
@@ -64,8 +73,8 @@ def tile_pace_nodagseq_kernel(tc, table, bnode, pos, wv, bv, wo, bo, offs, out):
         for hb in range(NB):
             nc.vector.tensor_scalar_add(v_sb[hb][:], v_ps[hb][:], bv_sb[:, hb : hb + 1])
 
-        for hb in range(NB):
-            for mb in range(NB):
+        for mb in range(NB):
+            for hb in range(NB):
                 nc.tensor.matmul(
                     out_ps[mb][:], wo_sb[:, hb, block(mb)], v_sb[hb][:], start=False, stop=(hb == NB - 1)
                 )

@@ -7,9 +7,6 @@ N = 128
 NH = 256
 NB = NH // P
 
-WARM_COLUMNS = 512
-WARM_MATMULS = 4
-
 FLOPS = 2 * 2 * NH * NH * N
 
 BF16, F32, U16 = mybir.dt.bfloat16, mybir.dt.float32, mybir.dt.uint16
@@ -39,20 +36,14 @@ def tile_pace_nodagseq_kernel(tc, table, bnode, pos, wv, bv, wo, bo, offs, out):
         nc.scalar.dma_start(bnode_sb[:], bnode)
         nc.sync.dma_start(offsets[:], offs)
         nc.scalar.dma_start(wv_sb[:], wv.rearrange("(b p) h -> p b h", p=P))
+        with nc.allow_non_contiguous_dma(reason="a bias: one float32 to a partition and block"):
+            nc.sync.dma_start(bv_sb[:], bv.rearrange("(b p) o -> p (b o)", p=P))
+            nc.scalar.dma_start(bo_sb[:], bo.rearrange("(b p) o -> p (b o)", p=P))
         nc.sync.dma_start(pos_sb[:], pos)
         nc.sync.dma_start(wo_sb[:], wo.rearrange("(b p) m -> p b m", p=P))
-        with nc.allow_non_contiguous_dma(reason="a bias: one float32 to a partition and block"):
-            nc.scalar.dma_start(bv_sb[:], bv.rearrange("(b p) o -> p (b o)", p=P))
-            nc.scalar.dma_start(bo_sb[:], bo.rearrange("(b p) o -> p (b o)", p=P))
 
         identity = held.tile([P, P], BF16, name="identity")
         make_identity(nc, identity[:])
-
-        warm_sb = held.tile([P, WARM_COLUMNS], BF16, name="warm_sb")
-        warm_ps = psum.tile([P, WARM_COLUMNS], F32, name="warm_ps")
-        nc.vector.memset(warm_sb[:], 0.0)
-        for i in range(WARM_MATMULS):
-            nc.tensor.matmul(warm_ps[:], warm_sb[:, 0:P], warm_sb[:], start=True, stop=True)
 
         feat = held.tile([P, S], BF16, name="feat")
         nc.vector.tensor_scalar(feat[:], table_sb[:], bnode_sb[:, 0:1], 0.0, op0=ADD, op1=MAX)

@@ -36,11 +36,11 @@ def tile_pace_nodagseq_kernel(tc, table, bnode, pos, wv, bv, wo, bo, offs, out):
         nc.scalar.dma_start(bnode_sb[:], bnode)
         nc.sync.dma_start(offsets[:], offs)
         nc.scalar.dma_start(wv_sb[:], wv.rearrange("(b p) h -> p b h", p=P))
+        nc.sync.dma_start(pos_sb[:], pos)
+        nc.scalar.dma_start(wo_sb[:], wo.rearrange("(b p) m -> p b m", p=P))
         with nc.allow_non_contiguous_dma(reason="a bias: one float32 to a partition and block"):
             nc.sync.dma_start(bv_sb[:], bv.rearrange("(b p) o -> p (b o)", p=P))
             nc.scalar.dma_start(bo_sb[:], bo.rearrange("(b p) o -> p (b o)", p=P))
-        nc.sync.dma_start(pos_sb[:], pos)
-        nc.sync.dma_start(wo_sb[:], wo.rearrange("(b p) m -> p b m", p=P))
 
         identity = held.tile([P, P], BF16, name="identity")
         make_identity(nc, identity[:])

@@ -35,12 +35,12 @@ def tile_pace_nodagseq_kernel(tc, table, bnode, pos, wv, bv, wo, bo, offs, out):
         nc.sync.dma_start(table_sb[:], table)
         nc.scalar.dma_start(bnode_sb[:], bnode)
         nc.sync.dma_start(offsets[:], offs)
-        nc.scalar.dma_start(wv_sb[:], wv.rearrange("(b p) h -> p b h", p=P))
-        nc.sync.dma_start(pos_sb[:], pos)
-        nc.scalar.dma_start(wo_sb[:], wo.rearrange("(b p) m -> p b m", p=P))
         with nc.allow_non_contiguous_dma(reason="a bias: one float32 to a partition and block"):
             nc.sync.dma_start(bv_sb[:], bv.rearrange("(b p) o -> p (b o)", p=P))
             nc.scalar.dma_start(bo_sb[:], bo.rearrange("(b p) o -> p (b o)", p=P))
+        nc.scalar.dma_start(wv_sb[:], wv.rearrange("(b p) h -> p b h", p=P))
+        nc.sync.dma_start(pos_sb[:], pos)
+        nc.sync.dma_start(wo_sb[:], wo.rearrange("(b p) m -> p b m", p=P))
 
         identity = held.tile([P, P], BF16, name="identity")
         make_identity(nc, identity[:])

@@ -35,11 +35,11 @@ def tile_pace_nodagseq_kernel(tc, table, bnode, pos, wv, bv, wo, bo, offs, out):
         nc.sync.dma_start(table_sb[:], table)
         nc.scalar.dma_start(bnode_sb[:], bnode)
         nc.sync.dma_start(offsets[:], offs)
+        nc.sync.dma_start(pos_sb[:], pos)
         with nc.allow_non_contiguous_dma(reason="a bias: one float32 to a partition and block"):
             nc.sync.dma_start(bv_sb[:], bv.rearrange("(b p) o -> p (b o)", p=P))
             nc.scalar.dma_start(bo_sb[:], bo.rearrange("(b p) o -> p (b o)", p=P))
         nc.scalar.dma_start(wv_sb[:], wv.rearrange("(b p) h -> p b h", p=P))
-        nc.sync.dma_start(pos_sb[:], pos)
         nc.sync.dma_start(wo_sb[:], wo.rearrange("(b p) m -> p b m", p=P))
 
         identity = held.tile([P, P], BF16, name="identity")

@@ -34,12 +34,12 @@ def tile_pace_nodagseq_kernel(tc, table, bnode, pos, wv, bv, wo, bo, offs, out):
 
         nc.sync.dma_start(table_sb[:], table)
         nc.scalar.dma_start(bnode_sb[:], bnode)
-        nc.sync.dma_start(offsets[:], offs)
         nc.sync.dma_start(pos_sb[:], pos)
+        nc.scalar.dma_start(wv_sb[:], wv.rearrange("(b p) h -> p b h", p=P))
+        nc.sync.dma_start(offsets[:], offs)
         with nc.allow_non_contiguous_dma(reason="a bias: one float32 to a partition and block"):
             nc.sync.dma_start(bv_sb[:], bv.rearrange("(b p) o -> p (b o)", p=P))
             nc.scalar.dma_start(bo_sb[:], bo.rearrange("(b p) o -> p (b o)", p=P))
-        nc.scalar.dma_start(wv_sb[:], wv.rearrange("(b p) h -> p b h", p=P))
         nc.sync.dma_start(wo_sb[:], wo.rearrange("(b p) m -> p b m", p=P))
 
         identity = held.tile([P, P], BF16, name="identity")

@@ -72,5 +72,5 @@ def tile_pace_nodagseq_kernel(tc, table, bnode, pos, wv, bv, wo, bo, offs, out):
         out_sb = [held.tile([P, N], F32, name=f"out_sb{mb}") for mb in range(NB)]
         for mb in range(NB):
             nc.vector.tensor_scalar_add(out_sb[mb][:], out_ps[mb][:], bo_sb[:, mb : mb + 1])
-        nc.sync.dma_start(out[block(0), :], out_sb[0][:])
-        nc.scalar.dma_start(out[block(1), :], out_sb[1][:])
+        nc.scalar.dma_start(out[block(0), :], out_sb[0][:])
+        nc.sync.dma_start(out[block(1), :], out_sb[1][:])

@@ -35,12 +35,14 @@ def tile_pace_nodagseq_kernel(tc, table, bnode, pos, wv, bv, wo, bo, offs, out):
         nc.sync.dma_start(table_sb[:], table)
         nc.scalar.dma_start(bnode_sb[:], bnode)
         nc.sync.dma_start(pos_sb[:], pos)
-        nc.scalar.dma_start(wv_sb[:], wv.rearrange("(b p) h -> p b h", p=P))
+        nc.scalar.dma_start(wv_sb[:, 1, :], wv[block(1), :])
         nc.sync.dma_start(offsets[:], offs)
+        nc.scalar.dma_start(wv_sb[:, 0, :], wv[block(0), :])
         with nc.allow_non_contiguous_dma(reason="a bias: one float32 to a partition and block"):
             nc.sync.dma_start(bv_sb[:], bv.rearrange("(b p) o -> p (b o)", p=P))
-            nc.scalar.dma_start(bo_sb[:], bo.rearrange("(b p) o -> p (b o)", p=P))
         nc.sync.dma_start(wo_sb[:], wo.rearrange("(b p) m -> p b m", p=P))
+        with nc.allow_non_contiguous_dma(reason="a bias: one float32 to a partition and block"):
+            nc.sync.dma_start(bo_sb[:], bo.rearrange("(b p) o -> p (b o)", p=P))
 
         identity = held.tile([P, P], BF16, name="identity")
         make_identity(nc, identity[:])

@@ -39,8 +39,8 @@ def tile_pace_nodagseq_kernel(tc, table, bnode, pos, wv, bv, wo, bo, offs, out):
         nc.sync.dma_start(offsets[:], offs)
         nc.scalar.dma_start(wv_sb[:, 0, :], wv[block(0), :])
         with nc.allow_non_contiguous_dma(reason="a bias: one float32 to a partition and block"):
-            nc.sync.dma_start(bv_sb[:], bv.rearrange("(b p) o -> p (b o)", p=P))
-        nc.sync.dma_start(wo_sb[:], wo.rearrange("(b p) m -> p b m", p=P))
+            nc.sync.dma_start(bv_sb[:], bv.rearrange("(p b) o -> p (b o)", b=NB))
+        nc.sync.dma_start(wo_sb[:], wo.rearrange("(p b) m -> p b m", b=NB))
         with nc.allow_non_contiguous_dma(reason="a bias: one float32 to a partition and block"):
             nc.sync.dma_start(bo_sb[:], bo.rearrange("(b p) o -> p (b o)", p=P))
 
@@ -52,10 +52,10 @@ def tile_pace_nodagseq_kernel(tc, table, bnode, pos, wv, bv, wo, bo, offs, out):
 
         v_ps = [psum.tile([P, N], F32, name=f"v_ps{hb}") for hb in range(NB)]
         for hb in range(NB):
-            nc.tensor.matmul(v_ps[hb][:], wv_sb[:, 1, block(hb)], pos_sb[:], start=True, stop=False)
+            nc.tensor.matmul(v_ps[hb][:], wv_sb[:, 1, hb::NB], pos_sb[:], start=True, stop=False)
         for hb in range(NB):
             nc.tensor.matmul(
-                v_ps[hb][:], wv_sb[:, 0, block(hb)], feat[:].indirect(offsets[:]), start=False, stop=True
+                v_ps[hb][:], wv_sb[:, 0, hb::NB], feat[:].indirect(offsets[:]), start=False, stop=True
             )
 
         out_ps = [psum.tile([P, N], F32, name=f"out_ps{mb}") for mb in range(NB)]

import concourse.mybir as mybir
from concourse.masks import make_identity

P = 128
S = 256
N = 128
NH = 256
NB = NH // P

FLOPS = 2 * 2 * NH * NH * N

BF16, F32, U16 = mybir.dt.bfloat16, mybir.dt.float32, mybir.dt.uint16
ADD, MAX = mybir.AluOpType.add, mybir.AluOpType.max


def block(b):
    return slice(b * P, (b + 1) * P)


def tile_pace_nodagseq_kernel(tc, table, bnode, pos, wv, bv, wo, bo, offs, out):
    nc = tc.nc
    with (
        tc.tile_pool(name="held", bufs=1) as held,
        tc.psum_pool(name="psum", bufs=1) as psum,
    ):
        offsets = held.tile([P, N // 16], U16, name="offsets")
        table_sb = held.tile([P, S], BF16, name="table_sb")
        bnode_sb = held.tile([P, 1], F32, name="bnode_sb")
        pos_sb = held.tile([P, N], BF16, name="pos_sb")
        wv_sb = held.tile([P, NB, NH], BF16, name="wv_sb")
        wo_sb = held.tile([P, NB, NH], BF16, name="wo_sb")
        bv_sb = held.tile([P, NB], F32, name="bv_sb")
        bo_sb = held.tile([P, NB], F32, name="bo_sb")

        nc.sync.dma_start(table_sb[:], table)
        nc.scalar.dma_start(bnode_sb[:], bnode)
        nc.sync.dma_start(pos_sb[:], pos)
        nc.scalar.dma_start(wv_sb[:, 1, :], wv[block(1), :])
        nc.sync.dma_start(offsets[:], offs)
        nc.scalar.dma_start(wv_sb[:, 0, :], wv[block(0), :])
        with nc.allow_non_contiguous_dma(reason="a bias: one float32 to a partition and block"):
            nc.sync.dma_start(bv_sb[:], bv.rearrange("(p b) o -> p (b o)", b=NB))
        nc.sync.dma_start(wo_sb[:], wo.rearrange("(p b) m -> p b m", b=NB))
        with nc.allow_non_contiguous_dma(reason="a bias: one float32 to a partition and block"):
            nc.sync.dma_start(bo_sb[:], bo.rearrange("(b p) o -> p (b o)", p=P))

        identity = held.tile([P, P], BF16, name="identity")
        make_identity(nc, identity[:])

        feat = held.tile([P, S], BF16, name="feat")
        nc.vector.tensor_scalar(feat[:], table_sb[:], bnode_sb[:, 0:1], 0.0, op0=ADD, op1=MAX)

        v_ps = [psum.tile([P, N], F32, name=f"v_ps{hb}") for hb in range(NB)]
        for hb in range(NB):
            nc.tensor.matmul(v_ps[hb][:], wv_sb[:, 1, hb::NB], pos_sb[:], start=True, stop=False)
        for hb in range(NB):
            nc.tensor.matmul(
                v_ps[hb][:], wv_sb[:, 0, hb::NB], feat[:].indirect(offsets[:]), start=False, stop=True
            )

        out_ps = [psum.tile([P, N], F32, name=f"out_ps{mb}") for mb in range(NB)]
        nc.tensor.matmul(out_ps[0][:], identity[:], feat[:].indirect(offsets[:]), start=True, stop=False)
        nc.tensor.matmul(out_ps[1][:], identity[:], pos_sb[:], start=True, stop=False)

        v_sb = [held.tile([P, N], BF16, name=f"v_sb{hb}") for hb in range(NB)]
        for hb in range(NB):
            nc.vector.tensor_scalar_add(v_sb[hb][:], v_ps[hb][:], bv_sb[:, hb : hb + 1])

        for mb in range(NB):
            for hb in range(NB):
                nc.tensor.matmul(
                    out_ps[mb][:], wo_sb[:, hb, block(mb)], v_sb[hb][:], start=False, stop=(hb == NB - 1)
                )
        out_sb = [held.tile([P, N], F32, name=f"out_sb{mb}") for mb in range(NB)]
        for mb in range(NB):
            nc.vector.tensor_scalar_add(out_sb[mb][:], out_ps[mb][:], bo_sb[:, mb : mb + 1])
        nc.scalar.dma_start(out[block(0), :], out_sb[0][:])
        nc.sync.dma_start(out[block(1), :], out_sb[1][:])
